import numpy as np
import ml_dtypes


def mxq(x, axis, fmt="e4m3"):
    dtype, down = {"e4m3": (ml_dtypes.float8_e4m3fn, 7), "e5m2": (ml_dtypes.float8_e5m2, 14)}[fmt]
    v = np.moveaxis(np.asarray(x, np.float32).astype(ml_dtypes.bfloat16).astype(np.float64), axis, -1)
    blocks = v.reshape(v.shape[:-1] + (-1, 32))
    amax = np.abs(blocks).max(-1, keepdims=True)
    byte = np.maximum(np.where(amax > 0, np.frexp(amax)[1] - 1 + 127, 0) - down, 1)
    scale = np.exp2(byte - 127.0)
    codes = (blocks / scale).astype(np.float32).astype(dtype).astype(np.float64)
    return np.moveaxis((codes * scale).reshape(v.shape), -1, axis)


WIDE = False


def mx_kscale(k):
    if not WIDE:
        return np.ones(k)
    levels = np.array([10, -10, 5, -5, 0])
    if k % 512:
        return np.exp2(np.random.permutation(np.resize(levels, k // 32))).repeat(32)
    a = np.empty((k // 512, 16))
    for p in range(k // 512):
        a[p, :8] = np.random.permutation(np.resize(levels, 8))
        for g in range(8):
            far = levels[np.abs(levels - a[p, g]) >= 10]
            a[p, g + 8] = far[np.random.randint(len(far))]
    return np.exp2(a.ravel()).repeat(32)


BF16 = ml_dtypes.bfloat16


def bf(x):
    return np.asarray(x, np.float32).astype(BF16)


def f64(x):
    return np.asarray(x).astype(np.float64)


B, D, S, A, H, G = 4096, 512, 1024, 128, 512, 1
DG = D // G


def silu(v):
    return v / (1.0 + np.exp(-v))


def sigmoid(v):
    return 1.0 / (1.0 + np.exp(-v))


def setup_inputs():
    n = np.random.standard_normal
    t = mx_kscale(D)
    return {"y_dyn": bf(silu(n((B, D))) * t), "deter": bf(n((B, D))),
            "gru_W": bf(n((G, DG, 3 * DG)) * 2.0 / np.sqrt(DG) / t.reshape(G, DG)[:, :, None]), "gru_b": bf(n(3 * D) * 0.2)}


def reference(y_dyn, deter, gru_W, gru_b):
    yg = f64(y_dyn).reshape(B, G, DG).transpose(1, 0, 2)
    z = mxq(yg, 2, "e4m3") @ mxq(f64(gru_W), 1, "e4m3")
    z = z.transpose(1, 0, 2).reshape(B, 3 * D) + f64(gru_b)
    reset, cand, update = z[:, :D], z[:, D:2 * D], z[:, 2 * D:]
    reset = sigmoid(reset)
    cand = np.tanh(reset * cand)
    update = sigmoid(update - 1.0)
    return update * cand + (1.0 - update) * f64(deter)

@@ -1,0 +1,246 @@
+from contextlib import ExitStack
+
+import concourse.mybir as mybir
+from concourse.masks import make_identity
+
+FLOPS = 2 * 4096 * 512 * 1536
+
+F32 = mybir.dt.float32
+BF16 = mybir.dt.bfloat16
+U32 = mybir.dt.uint32
+U8 = mybir.dt.uint8
+FP8X4 = mybir.dt.float8_e4m3fn_x4
+ACT = mybir.ActivationFunctionType
+ALU = mybir.AluOpType
+
+P = 128
+N = 512
+ROUNDS = 8
+STRIPS = 4 * ROUNDS
+GATE_R, GATE_C, GATE_U = 0, 1, 2
+
+
+def tile_blockgrucell_pb_t_kernel(tc, y_dyn, deter, gru_W, gru_b, out):
+    nc = tc.nc
+    y_rows = y_dyn.rearrange("(g p i) k -> g p (i k)", p=P, i=4)
+    d_rows = deter.rearrange("(g p i) c -> g p (i c)", p=P, i=4)
+    o_rows = out.rearrange("(g p i) c -> g p i c", p=P, i=4)
+
+    with ExitStack() as ctx:
+        keep = ctx.enter_context(tc.tile_pool(name="keep", bufs=1))
+        work = ctx.enter_context(tc.tile_pool(name="work", bufs=3))
+        psum = ctx.enter_context(tc.psum_pool(name="psum", bufs=1))
+        ctx.enter_context(tc.manual_schedule())
+
+        def bank(tag, bufs):
+            return psum.tile([P, N], F32, name=tag, tag=tag, bufs=bufs)
+
+        def strip_tile(tag, bufs):
+            return work.tile([P, N], F32, name=tag, tag=tag, bufs=bufs)
+
+        ident = keep.tile([P, P], F32, name="ident")
+        make_identity(nc, ident[:])
+        b_rows = keep.tile([P, 256], BF16, name="b_rows")
+        nc.vector.memset(b_rows[:], 0.0)
+        nc.scalar.dma_start(out=b_rows[0:6, :], in_=gru_b.rearrange("(m c) -> m c", c=256))
+        warm = keep.tile([P, 2], F32, name="warm")
+        nc.vector.memset(warm[:], 0.0)
+        nc.scalar.activation(out=warm[:, 1:2], in_=warm[:, 0:1], func=ACT.Sigmoid)
+
+        y_sb = [keep.tile([P, 4 * 512], BF16, name="y%d" % g) for g in range(ROUNDS)]
+        d_sb = [keep.tile([P, 4 * 512], BF16, name="d%d" % g) for g in range(ROUNDS)]
+        w_raw = keep.tile([P, 4, 1536], BF16, name="w_raw")
+        for half in range(2):
+            cols = slice(1024 * half, 1024 * half + 1024)
+            nc.sync.dma_start(out=y_sb[0][:, cols], in_=y_rows[0][:, cols])
+        for h in range(2):
+            for gate in (GATE_R, GATE_U, GATE_C):
+                cols = slice(512 * gate + 256 * h, 512 * gate + 256 * h + 256)
+                nc.sync.dma_start(out=w_raw[:, :, cols], in_=gru_W[0, :, cols].rearrange("(q t) c -> q t c", t=4))
+        for g in range(ROUNDS):
+            if g + 1 < ROUNDS:
+                nc.sync.dma_start(out=y_sb[g + 1][:], in_=y_rows[g + 1])
+            nc.sync.dma_start(out=d_sb[g][:], in_=d_rows[g])
+
+        b_bank = bank("yT", 1)
+        nc.tensor.transpose(b_bank[:, 0:P], b_rows[:].bitcast(F32), ident[:])
+        bias = keep.tile([P, 12], F32, name="bias")
+        nc.vector.tensor_copy(out=bias[:], in_=b_bank[:].bitcast(BF16)[:, 0:12])
+        nc.vector.tensor_scalar_add(
+            out=bias[:, 4 * GATE_U : 4 * GATE_U + 4], in0=bias[:, 4 * GATE_U : 4 * GATE_U + 4], scalar1=-1.0
+        )
+
+        def bias_of(gate, x):
+            column = 4 * gate + x % 4
+            return bias[:, column : column + 1]
+
+        w_grouped = keep.tile([P, 6 * 1024], BF16, name="w_grouped", align_bytes=64)
+        w_codes = keep.tile([P, 6 * 256], U32, name="w_codes", align_bytes=64)
+        w_scales = keep.tile([P, 6 * 256], U8, name="w_scales", align_bytes=64)
+
+        def regroup_weights(copy, h, gate):
+            slot = 3 * h + gate
+            first = 512 * gate + 256 * h
+            copy(
+                out=w_grouped[:, 1024 * slot : 1024 * slot + 1024].rearrange("p (e q t) -> p e q t", e=2, t=4),
+                in_=w_raw[:, :, first : first + 256].rearrange("p t (q e) -> p e q t", e=2),
+            )
+
+        def quantise_weights(h, gate):
+            slot = 3 * h + gate
+            nc.vector.quantize_mx(
+                out=w_codes[:, 256 * slot : 256 * slot + 256].bitcast(FP8X4),
+                scales=w_scales[:, 256 * slot : 256 * slot + 256],
+                in_=w_grouped[:, 1024 * slot : 1024 * slot + 1024],
+            )
+
+        live = {}
+
+        def transpose_y(g, half):
+            live["yT", g, half] = bank("back", 2) if g == 0 else bank("yT", 1)
+            words = y_sb[g][:].bitcast(F32)
+            for i in range(2):
+                for u in range(2):
+                    row = 256 * (2 * half + i)
+                    dst = 128 * (2 * i + u)
+                    nc.tensor.transpose(live["yT", g, half][:, dst : dst + P], words[:, row + u : row + 256 : 2], ident[:])
+
+        def regroup_y(g, half):
+            if half == 0:
+                live["y_grouped", g] = work.tile([P, 4 * N], BF16, name="y_grouped", tag="y_grouped", bufs=2, align_bytes=64)
+            words = live["y_grouped", g][:].bitcast(F32).rearrange("p (n u) -> p n u", u=2)
+            nc.scalar.copy(
+                out=words[:, 256 * half : 256 * half + 256, :].rearrange("p (i r) u -> p i r u", i=2),
+                in_=live["yT", g, half][:].rearrange("p (i u r) -> p i r u", i=2, u=2),
+            )
+
+        def quantise_y(g, half):
+            if half == 0:
+                live["y_codes", g] = work.tile([P, N], U32, name="y_codes", tag="y_codes", bufs=2, align_bytes=64)
+                live["y_scales", g] = work.tile([P, N], U8, name="y_scales", tag="y_scales", bufs=2, align_bytes=64)
+            cols = slice(256 * half, 256 * half + 256)
+            nc.vector.quantize_mx(
+                out=live["y_codes", g][:, cols].bitcast(FP8X4),
+                scales=live["y_scales", g][:, cols],
+                in_=live["y_grouped", g][:, 1024 * half : 1024 * half + 1024],
+            )
+
+        def project(x):
+            g, h, e = x // 4, x // 2 % 2, x % 2
+            for gate in (GATE_R, GATE_U, GATE_C):
+                first = 256 * (3 * h + gate) + P * e
+                live["z", gate, x] = bank("z", 4)
+                nc.tensor.matmul_mx(
+                    out=live["z", gate, x][:],
+                    lhsT=w_codes[:, first : first + P].bitcast(FP8X4),
+                    lhsT_scale=w_scales[:, first : first + P],
+                    rhs=live["y_codes", g][:].bitcast(FP8X4),
+                    rhs_scale=live["y_scales", g][:],
+                    start=True,
+                    stop=True,
+                )
+
+        def gates(x):
+            live["reset", x] = strip_tile("reset", 3)
+            live["update", x] = strip_tile("update", 5)
+            live["product", x] = strip_tile("product", 3)
+            nc.scalar.activation(
+                out=live["reset", x][:], in_=live["z", GATE_R, x][:], func=ACT.Sigmoid, bias=bias_of(GATE_R, x)
+            )
+            nc.scalar.activation(
+                out=live["update", x][:], in_=live["z", GATE_U, x][:], func=ACT.Sigmoid, bias=bias_of(GATE_U, x)
+            )
+            nc.vector.scalar_tensor_tensor(
+                out=live["product", x][:],
+                in0=live["z", GATE_C, x][:],
+                scalar=bias_of(GATE_C, x),
+                in1=live["reset", x][:],
+                op0=ALU.add,
+                op1=ALU.mult,
+            )
+
+        def candidate(x):
+            live["cand", x] = strip_tile("cand", 3)
+            nc.scalar.activation(out=live["cand", x][:], in_=live["product", x][:], func=ACT.Tanh)
+
+        def transpose_deter(pair):
+            g, h = pair // 2, pair % 2
+            live["deterT", pair] = bank("deterT", 1)
+            words = d_sb[g][:].bitcast(F32)
+            for i in range(4):
+                src = 256 * i + P * h
+                nc.tensor.transpose(live["deterT", pair][:, P * i : P * i + P], words[:, src : src + P], ident[:])
+
+        def blend(x):
+            live["diff", x] = strip_tile("diff", 3)
+            live["step", x] = strip_tile("step", 5)
+            nc.vector.tensor_tensor(
+                out=live["diff", x][:],
+                in0=live["cand", x][:],
+                in1=live["deterT", x // 2][:].bitcast(BF16).rearrange("p (n e) -> p e n", e=2)[:, x % 2, :],
+                op=ALU.subtract,
+            )
+            engine = nc.vector if x == STRIPS - 1 else nc.gpsimd
+            engine.tensor_tensor(out=live["step", x][:], in0=live["update", x][:], in1=live["diff", x][:], op=ALU.mult)
+
+        def transpose_back(x):
+            even = x - x % 2
+            live["back", x] = bank("back", 2)
+            for i in range(2):
+                for e in range(2):
+                    src = P * (2 * (x % 2) + i)
+                    dst = P * (2 * i + e)
+                    nc.tensor.transpose(live["back", x][:, dst : dst + P], live["step", even + e][:, src : src + P], ident[:])
+
+        def finish(x):
+            g, h, slots = x // 4, x // 2 % 2, slice(2 * (x % 2), 2 * (x % 2) + 2)
+            cols = slice(256 * h, 256 * h + 256)
+            result = strip_tile("result", 4)
+            nc.vector.tensor_tensor(
+                out=result[:].rearrange("p (i q e) -> p i q e", i=2, e=2),
+                in0=live["back", x][:].rearrange("p (i e q) -> p i q e", i=2, e=2),
+                in1=d_sb[g][:].rearrange("p (i c) -> p i c", i=4)[:, slots, cols].rearrange("p i (q e) -> p i q e", e=2),
+                op=ALU.add,
+            )
+            nc.sync.dma_start(out=o_rows[g][:, slots, cols], in_=result[:].rearrange("p (i c) -> p i c", i=2))
+
+        transpose_y(0, 0)
+        transpose_y(0, 1)
+        regroup_y(0, 0)
+        regroup_y(0, 1)
+        regroup_weights(nc.vector.tensor_copy, 0, GATE_R)
+        quantise_weights(0, GATE_R)
+        quantise_y(0, 0)
+        quantise_y(0, 1)
+        regroup_weights(nc.scalar.copy, 0, GATE_U)
+        regroup_weights(nc.vector.tensor_copy, 0, GATE_C)
+        quantise_weights(0, GATE_U)
+        quantise_weights(0, GATE_C)
+        for gate in (GATE_R, GATE_U, GATE_C):
+            regroup_weights(nc.vector.tensor_copy, 1, gate)
+            quantise_weights(1, gate)
+
+        def in_range(x):
+            return 0 <= x < STRIPS
+
+        for s in range(-2, STRIPS + 4):
+            if in_range(s - 1):
+                blend(s - 1)
+            if 4 <= s + 4 < STRIPS and (s + 4) % 4 < 2:
+                quantise_y((s + 4) // 4, (s + 4) % 4)
+            if in_range(s + 1):
+                gates(s + 1)
+            if 4 <= s + 5 < STRIPS and (s + 5) % 4 < 2:
+                regroup_y((s + 5) // 4, (s + 5) % 4)
+            if in_range(s - 4):
+                finish(s - 4)
+            if in_range(s):
+                candidate(s)
+            if in_range(s + 2):
+                project(s + 2)
+            if 4 <= s + 6 < STRIPS and (s + 6) % 4 < 2:
+                transpose_y((s + 6) // 4, (s + 6) % 4)
+            if in_range(s) and s % 2 == 0:
+                transpose_deter(s // 2)
+            if in_range(s - 3):
+                transpose_back(s - 3)

@@ -42,33 +42,36 @@ def tile_blockgrucell_pb_t_kernel(tc, y_dyn, deter, gru_W, gru_b, out):
         make_identity(nc, ident[:])
         b_rows = keep.tile([P, 256], BF16, name="b_rows")
         nc.vector.memset(b_rows[:], 0.0)
-        nc.scalar.dma_start(out=b_rows[0:6, :], in_=gru_b.rearrange("(m c) -> m c", c=256))
         warm = keep.tile([P, 2], F32, name="warm")
         nc.vector.memset(warm[:], 0.0)
         nc.scalar.activation(out=warm[:, 1:2], in_=warm[:, 0:1], func=ACT.Sigmoid)
 
         y_sb = [keep.tile([P, 4 * 512], BF16, name="y%d" % g) for g in range(ROUNDS)]
         d_sb = [keep.tile([P, 4 * 512], BF16, name="d%d" % g) for g in range(ROUNDS)]
-        w_raw = keep.tile([P, 4, 1536], BF16, name="w_raw")
+        w_raw = {}
         for half in range(2):
             cols = slice(1024 * half, 1024 * half + 1024)
             nc.sync.dma_start(out=y_sb[0][:, cols], in_=y_rows[0][:, cols])
+        nc.sync.dma_start(out=b_rows[0:6, :], in_=gru_b.rearrange("(m c) -> m c", c=256))
         for h in range(2):
             for gate in (GATE_R, GATE_U, GATE_C):
                 cols = slice(512 * gate + 256 * h, 512 * gate + 256 * h + 256)
-                nc.sync.dma_start(out=w_raw[:, :, cols], in_=gru_W[0, :, cols].rearrange("(q t) c -> q t c", t=4))
+                w_raw[h, gate] = keep.tile([P, 4, 256], BF16, name="w_raw_%d%d" % (h, gate))
+                nc.sync.dma_start(out=w_raw[h, gate][:], in_=gru_W[0, :, cols].rearrange("(q t) c -> q t c", t=4))
         for g in range(ROUNDS):
             if g + 1 < ROUNDS:
                 nc.sync.dma_start(out=y_sb[g + 1][:], in_=y_rows[g + 1])
             nc.sync.dma_start(out=d_sb[g][:], in_=d_rows[g])
 
-        b_bank = bank("yT", 1)
-        nc.tensor.transpose(b_bank[:, 0:P], b_rows[:].bitcast(F32), ident[:])
         bias = keep.tile([P, 12], F32, name="bias")
-        nc.vector.tensor_copy(out=bias[:], in_=b_bank[:].bitcast(BF16)[:, 0:12])
-        nc.vector.tensor_scalar_add(
-            out=bias[:, 4 * GATE_U : 4 * GATE_U + 4], in0=bias[:, 4 * GATE_U : 4 * GATE_U + 4], scalar1=-1.0
-        )
+
+        def make_bias():
+            b_bank = bank("yT", 1)
+            nc.tensor.transpose(b_bank[:, 0:P], b_rows[:].bitcast(F32), ident[:])
+            nc.vector.tensor_copy(out=bias[:], in_=b_bank[:].bitcast(BF16)[:, 0:12])
+            nc.vector.tensor_scalar_add(
+                out=bias[:, 4 * GATE_U : 4 * GATE_U + 4], in0=bias[:, 4 * GATE_U : 4 * GATE_U + 4], scalar1=-1.0
+            )
 
         def bias_of(gate, x):
             column = 4 * gate + x % 4
@@ -80,10 +83,9 @@ def tile_blockgrucell_pb_t_kernel(tc, y_dyn, deter, gru_W, gru_b, out):
 
         def regroup_weights(copy, h, gate):
             slot = 3 * h + gate
-            first = 512 * gate + 256 * h
             copy(
                 out=w_grouped[:, 1024 * slot : 1024 * slot + 1024].rearrange("p (e q t) -> p e q t", e=2, t=4),
-                in_=w_raw[:, :, first : first + 256].rearrange("p t (q e) -> p e q t", e=2),
+                in_=w_raw[h, gate][:].rearrange("p t (q e) -> p e q t", e=2),
             )
 
         def quantise_weights(h, gate):
@@ -206,6 +208,7 @@ def tile_blockgrucell_pb_t_kernel(tc, y_dyn, deter, gru_W, gru_b, out):
 
         transpose_y(0, 0)
         transpose_y(0, 1)
+        make_bias()
         regroup_y(0, 0)
         regroup_y(0, 1)
         regroup_weights(nc.vector.tensor_copy, 0, GATE_R)

@@ -111,7 +111,8 @@ def tile_blockgrucell_pb_t_kernel(tc, y_dyn, deter, gru_W, gru_b, out):
             if half == 0:
                 live["y_grouped", g] = work.tile([P, 4 * N], BF16, name="y_grouped", tag="y_grouped", bufs=2, align_bytes=64)
             words = live["y_grouped", g][:].bitcast(F32).rearrange("p (n u) -> p n u", u=2)
-            nc.scalar.copy(
+            copy = nc.vector.tensor_copy if half == 1 and 0 < g < 5 else nc.scalar.copy
+            copy(
                 out=words[:, 256 * half : 256 * half + 256, :].rearrange("p (i r) u -> p i r u", i=2),
                 in_=live["yT", g, half][:].rearrange("p (i u r) -> p i r u", i=2, u=2),
             )
@@ -226,23 +227,26 @@ def tile_blockgrucell_pb_t_kernel(tc, y_dyn, deter, gru_W, gru_b, out):
         def in_range(x):
             return 0 <= x < STRIPS
 
+        def y_stage(stage, s):
+            for g in range(1, ROUNDS):
+                for half in range(2):
+                    if s == max(4 * g - 7 + 2 * half, -2):
+                        stage(g, half)
+
         for s in range(-2, STRIPS + 4):
             if in_range(s - 1):
                 blend(s - 1)
-            if 4 <= s + 4 < STRIPS and (s + 4) % 4 < 2:
-                quantise_y((s + 4) // 4, (s + 4) % 4)
+            y_stage(quantise_y, s - 2)
             if in_range(s + 1):
                 gates(s + 1)
-            if 4 <= s + 5 < STRIPS and (s + 5) % 4 < 2:
-                regroup_y((s + 5) // 4, (s + 5) % 4)
+            y_stage(regroup_y, s - 1)
             if in_range(s - 4):
                 finish(s - 4)
             if in_range(s):
                 candidate(s)
             if in_range(s + 2):
                 project(s + 2)
-            if 4 <= s + 6 < STRIPS and (s + 6) % 4 < 2:
-                transpose_y((s + 6) // 4, (s + 6) % 4)
+            y_stage(transpose_y, s)
             if in_range(s) and s % 2 == 0:
                 transpose_deter(s // 2)
             if in_range(s - 3):

@@ -17,6 +17,7 @@ P = 128
 N = 512
 ROUNDS = 8
 STRIPS = 4 * ROUNDS
+SUMMED = (26, 27, 28, 29, 31)
 GATE_R, GATE_C, GATE_U = 0, 1, 2
 
 
@@ -40,6 +41,8 @@ def tile_blockgrucell_pb_t_kernel(tc, y_dyn, deter, gru_W, gru_b, out):
 
         ident = keep.tile([P, P], F32, name="ident")
         make_identity(nc, ident[:])
+        ident_bf16 = keep.tile([P, P], BF16, name="ident_bf16")
+        nc.vector.tensor_copy(out=ident_bf16[:], in_=ident[:])
         b_rows = keep.tile([P, 256], BF16, name="b_rows")
         nc.vector.memset(b_rows[:], 0.0)
         warm = keep.tile([P, 2], F32, name="warm")
@@ -177,34 +180,53 @@ def tile_blockgrucell_pb_t_kernel(tc, y_dyn, deter, gru_W, gru_b, out):
         def blend(x):
             live["diff", x] = strip_tile("diff", 3)
             live["step", x] = strip_tile("step", 5)
-            nc.vector.tensor_tensor(
-                out=live["diff", x][:],
-                in0=live["cand", x][:],
-                in1=live["deterT", x // 2][:].bitcast(BF16).rearrange("p (n e) -> p e n", e=2)[:, x % 2, :],
-                op=ALU.subtract,
-            )
-            engine = nc.vector if x == STRIPS - 1 else nc.gpsimd
-            engine.tensor_tensor(out=live["step", x][:], in0=live["update", x][:], in1=live["diff", x][:], op=ALU.mult)
+            last = x == STRIPS - 1
+            engine = nc.vector if last else nc.gpsimd
+            parts = [slice(0, 256), slice(256, 512)] if last else [slice(0, 512)]
+            for part in parts:
+                nc.vector.tensor_tensor(
+                    out=live["diff", x][:, part],
+                    in0=live["cand", x][:, part],
+                    in1=live["deterT", x // 2][:].bitcast(BF16).rearrange("p (n e) -> p e n", e=2)[:, x % 2, part],
+                    op=ALU.subtract,
+                )
+            for part in parts:
+                engine.tensor_tensor(
+                    out=live["step", x][:, part], in0=live["update", x][:, part], in1=live["diff", x][:, part], op=ALU.mult
+                )
 
         def transpose_back(x):
-            even = x - x % 2
-            live["back", x] = bank("back", 2)
+            g, h, even = x // 4, x // 2 % 2, x - x % 2
+            live["back", x] = bank("back", 2) if x < STRIPS - 4 else bank("z", 4)
             for i in range(2):
+                slot = 2 * (x % 2) + i
                 for e in range(2):
-                    src = P * (2 * (x % 2) + i)
-                    dst = P * (2 * i + e)
-                    nc.tensor.transpose(live["back", x][:, dst : dst + P], live["step", even + e][:, src : src + P], ident[:])
+                    dst = live["back", x][:, P * (2 * i + e) : P * (2 * i + e) + P]
+                    step = live["step", even + e][:, P * slot : P * slot + P]
+                    if x in SUMMED:
+                        first = 512 * slot + 256 * h + e
+                        nc.tensor.matmul(
+                            dst, lhsT=ident_bf16[:], rhs=d_sb[g][:, first : first + 255 : 2], start=True, stop=False
+                        )
+                        nc.tensor.matmul(dst, lhsT=step, rhs=ident[:], start=False, stop=True, is_transpose=True)
+                    else:
+                        nc.tensor.transpose(dst, step, ident[:])
 
         def finish(x):
             g, h, slots = x // 4, x // 2 % 2, slice(2 * (x % 2), 2 * (x % 2) + 2)
             cols = slice(256 * h, 256 * h + 256)
-            result = strip_tile("result", 4)
-            nc.vector.tensor_tensor(
-                out=result[:].rearrange("p (i q e) -> p i q e", i=2, e=2),
-                in0=live["back", x][:].rearrange("p (i e q) -> p i q e", i=2, e=2),
-                in1=d_sb[g][:].rearrange("p (i c) -> p i c", i=4)[:, slots, cols].rearrange("p i (q e) -> p i q e", e=2),
-                op=ALU.add,
-            )
+            result = strip_tile("result", 8)
+            back = live["back", x][:].rearrange("p (i e q) -> p i q e", i=2, e=2)
+            total = result[:].rearrange("p (i q e) -> p i q e", i=2, e=2)
+            if x in SUMMED:
+                nc.scalar.copy(out=total, in_=back)
+            else:
+                nc.vector.tensor_tensor(
+                    out=total,
+                    in0=back,
+                    in1=d_sb[g][:].rearrange("p (i c) -> p i c", i=4)[:, slots, cols].rearrange("p i (q e) -> p i q e", e=2),
+                    op=ALU.add,
+                )
             nc.sync.dma_start(out=o_rows[g][:, slots, cols], in_=result[:].rearrange("p (i c) -> p i c", i=2))
 
         transpose_y(0, 0)
@@ -240,10 +262,15 @@ def tile_blockgrucell_pb_t_kernel(tc, y_dyn, deter, gru_W, gru_b, out):
             if in_range(s + 1):
                 gates(s + 1)
             y_stage(regroup_y, s - 1)
-            if in_range(s - 4):
+            if in_range(s - 4) and s < STRIPS - 2:
                 finish(s - 4)
             if in_range(s):
                 candidate(s)
+            if s == STRIPS - 1:
+                finish(26)
+                finish(27)
+            if in_range(s - 4) and s >= STRIPS:
+                finish(s - 4)
             if in_range(s + 2):
                 project(s + 2)
             y_stage(transpose_y, s)

@@ -17,7 +17,7 @@ P = 128
 N = 512
 ROUNDS = 8
 STRIPS = 4 * ROUNDS
-SUMMED = (26, 27, 28, 29, 31)
+SUMMED = (26, 27, 28, 29, 30, 31)
 GATE_R, GATE_C, GATE_U = 0, 1, 2
 
 
@@ -41,12 +41,12 @@ def tile_blockgrucell_pb_t_kernel(tc, y_dyn, deter, gru_W, gru_b, out):
 
         ident = keep.tile([P, P], F32, name="ident")
         make_identity(nc, ident[:])
-        ident_bf16 = keep.tile([P, P], BF16, name="ident_bf16")
-        nc.vector.tensor_copy(out=ident_bf16[:], in_=ident[:])
         b_rows = keep.tile([P, 256], BF16, name="b_rows")
         nc.vector.memset(b_rows[:], 0.0)
         warm = keep.tile([P, 2], F32, name="warm")
         nc.vector.memset(warm[:], 0.0)
+        ident_bf16 = keep.tile([P, P], BF16, name="ident_bf16")
+        nc.vector.tensor_copy(out=ident_bf16[:], in_=ident[:])
         nc.scalar.activation(out=warm[:, 1:2], in_=warm[:, 0:1], func=ACT.Sigmoid)
 
         y_sb = [keep.tile([P, 4 * 512], BF16, name="y%d" % g) for g in range(ROUNDS)]
@@ -180,35 +180,58 @@ def tile_blockgrucell_pb_t_kernel(tc, y_dyn, deter, gru_W, gru_b, out):
         def blend(x):
             live["diff", x] = strip_tile("diff", 3)
             live["step", x] = strip_tile("step", 5)
-            last = x == STRIPS - 1
-            engine = nc.vector if last else nc.gpsimd
-            parts = [slice(0, 256), slice(256, 512)] if last else [slice(0, 512)]
-            for part in parts:
+
+            def subtract(part):
                 nc.vector.tensor_tensor(
                     out=live["diff", x][:, part],
                     in0=live["cand", x][:, part],
                     in1=live["deterT", x // 2][:].bitcast(BF16).rearrange("p (n e) -> p e n", e=2)[:, x % 2, part],
                     op=ALU.subtract,
                 )
-            for part in parts:
+
+            def multiply(engine, x, part):
                 engine.tensor_tensor(
                     out=live["step", x][:, part], in0=live["update", x][:, part], in1=live["diff", x][:, part], op=ALU.mult
                 )
 
-        def transpose_back(x):
-            g, h, even = x // 4, x // 2 % 2, x - x % 2
+            whole, halves = slice(0, 512), (slice(0, 256), slice(256, 512))
+            if x < STRIPS - 2:
+                subtract(whole)
+                multiply(nc.gpsimd, x, whole)
+            elif x == STRIPS - 2:
+                subtract(whole)
+            else:
+                multiply(nc.vector, x - 1, whole)
+                for part in halves:
+                    subtract(part)
+                for part in halves:
+                    multiply(nc.vector, x, part)
+
+        def open_sum(x):
+            g, h, slots = x // 4, x // 2 % 2, slice(2 * (x % 2), 2 * (x % 2) + 2)
             live["back", x] = bank("back", 2) if x < STRIPS - 4 else bank("z", 4)
+            rows = d_sb[g][:].rearrange("p (i c) -> p i c", i=4)[:, slots, 256 * h : 256 * h + 256]
+            nc.tensor.matmul(
+                live["back", x][:].rearrange("p (i e q) -> p i e q", i=2, e=2),
+                lhsT=ident_bf16[:],
+                rhs=rows.rearrange("p i (q e) -> p i e q", e=2),
+                start=True,
+                stop=False,
+            )
+
+        def transpose_back(x):
+            even = x - x % 2
+            if x not in SUMMED:
+                live["back", x] = bank("back", 2)
             for i in range(2):
                 slot = 2 * (x % 2) + i
                 for e in range(2):
                     dst = live["back", x][:, P * (2 * i + e) : P * (2 * i + e) + P]
                     step = live["step", even + e][:, P * slot : P * slot + P]
                     if x in SUMMED:
-                        first = 512 * slot + 256 * h + e
                         nc.tensor.matmul(
-                            dst, lhsT=ident_bf16[:], rhs=d_sb[g][:, first : first + 255 : 2], start=True, stop=False
+                            dst, lhsT=step, rhs=ident[:], start=False, stop=i == 1 and e == 1, is_transpose=True
                         )
-                        nc.tensor.matmul(dst, lhsT=step, rhs=ident[:], start=False, stop=True, is_transpose=True)
                     else:
                         nc.tensor.transpose(dst, step, ident[:])
 
@@ -219,7 +242,7 @@ def tile_blockgrucell_pb_t_kernel(tc, y_dyn, deter, gru_W, gru_b, out):
             back = live["back", x][:].rearrange("p (i e q) -> p i q e", i=2, e=2)
             total = result[:].rearrange("p (i q e) -> p i q e", i=2, e=2)
             if x in SUMMED:
-                nc.scalar.copy(out=total, in_=back)
+                (nc.vector.tensor_copy if x in (31,) else nc.scalar.copy)(out=total, in_=back)
             else:
                 nc.vector.tensor_tensor(
                     out=total,
@@ -276,5 +299,10 @@ def tile_blockgrucell_pb_t_kernel(tc, y_dyn, deter, gru_W, gru_b, out):
             y_stage(transpose_y, s)
             if in_range(s) and s % 2 == 0:
                 transpose_deter(s // 2)
+            if s - 3 in SUMMED[:2]:
+                open_sum(s - 3)
+            if s == STRIPS - 1:
+                for x in SUMMED[2:]:
+                    open_sum(x)
             if in_range(s - 3):
                 transpose_back(s - 3)

@@ -80,9 +80,9 @@ def tile_blockgrucell_pb_t_kernel(tc, y_dyn, deter, gru_W, gru_b, out):
             column = 4 * gate + x % 4
             return bias[:, column : column + 1]
 
-        w_grouped = keep.tile([P, 6 * 1024], BF16, name="w_grouped", align_bytes=64)
-        w_codes = keep.tile([P, 6 * 256], U32, name="w_codes", align_bytes=64)
-        w_scales = keep.tile([P, 6 * 256], U8, name="w_scales", align_bytes=64)
+        w_grouped = keep.tile([P, 6 * 1024], BF16, name="w_grouped", align_bytes=256)
+        w_codes = keep.tile([P, 6 * 256], U32, name="w_codes", align_bytes=256)
+        w_scales = keep.tile([P, 6 * 256], U8, name="w_scales", align_bytes=256)
 
         def regroup_weights(copy, h, gate):
             slot = 3 * h + gate
@@ -112,7 +112,7 @@ def tile_blockgrucell_pb_t_kernel(tc, y_dyn, deter, gru_W, gru_b, out):
 
         def regroup_y(g, half):
             if half == 0:
-                live["y_grouped", g] = work.tile([P, 4 * N], BF16, name="y_grouped", tag="y_grouped", bufs=2, align_bytes=64)
+                live["y_grouped", g] = work.tile([P, 4 * N], BF16, name="y_grouped", tag="y_grouped", bufs=2, align_bytes=256)
             words = live["y_grouped", g][:].bitcast(F32).rearrange("p (n u) -> p n u", u=2)
             copy = nc.vector.tensor_copy if half == 1 and 0 < g < 5 else nc.scalar.copy
             copy(
@@ -122,8 +122,8 @@ def tile_blockgrucell_pb_t_kernel(tc, y_dyn, deter, gru_W, gru_b, out):
 
         def quantise_y(g, half):
             if half == 0:
-                live["y_codes", g] = work.tile([P, N], U32, name="y_codes", tag="y_codes", bufs=2, align_bytes=64)
-                live["y_scales", g] = work.tile([P, N], U8, name="y_scales", tag="y_scales", bufs=2, align_bytes=64)
+                live["y_codes", g] = work.tile([P, N], U32, name="y_codes", tag="y_codes", bufs=2, align_bytes=256)
+                live["y_scales", g] = work.tile([P, N], U8, name="y_scales", tag="y_scales", bufs=2, align_bytes=256)
             cols = slice(256 * half, 256 * half + 256)
             nc.vector.quantize_mx(
                 out=live["y_codes", g][:, cols].bitcast(FP8X4),

@@ -69,7 +69,7 @@ def tile_blockgrucell_pb_t_kernel(tc, y_dyn, deter, gru_W, gru_b, out):
         bias = keep.tile([P, 12], F32, name="bias")
 
         def make_bias():
-            b_bank = bank("yT", 1)
+            b_bank = bank("z", 7)
             nc.tensor.transpose(b_bank[:, 0:P], b_rows[:].bitcast(F32), ident[:])
             nc.vector.tensor_copy(out=bias[:], in_=b_bank[:].bitcast(BF16)[:, 0:12])
             nc.vector.tensor_scalar_add(
@@ -87,8 +87,8 @@ def tile_blockgrucell_pb_t_kernel(tc, y_dyn, deter, gru_W, gru_b, out):
         def regroup_weights(copy, h, gate):
             slot = 3 * h + gate
             copy(
-                out=w_grouped[:, 1024 * slot : 1024 * slot + 1024].rearrange("p (e q t) -> p e q t", e=2, t=4),
-                in_=w_raw[h, gate][:].rearrange("p t (q e) -> p e q t", e=2),
+                out=w_grouped[:, 1024 * slot : 1024 * slot + 1024].rearrange("p (e c i t) -> p e c t i", e=2, i=4, t=4),
+                in_=w_raw[h, gate][:].rearrange("p t (c i e) -> p e c t i", i=4, e=2),
             )
 
         def quantise_weights(h, gate):
@@ -102,7 +102,7 @@ def tile_blockgrucell_pb_t_kernel(tc, y_dyn, deter, gru_W, gru_b, out):
         live = {}
 
         def transpose_y(g, half):
-            live["yT", g, half] = bank("back", 2) if g == 0 else bank("yT", 1)
+            live["yT", g, half] = bank("z", 7) if g == 0 else bank("z", 7)
             words = y_sb[g][:].bitcast(F32)
             for i in range(2):
                 for u in range(2):
@@ -135,7 +135,7 @@ def tile_blockgrucell_pb_t_kernel(tc, y_dyn, deter, gru_W, gru_b, out):
             g, h, e = x // 4, x // 2 % 2, x % 2
             for gate in (GATE_R, GATE_U, GATE_C):
                 first = 256 * (3 * h + gate) + P * e
-                live["z", gate, x] = bank("z", 4)
+                live["z", gate, x] = bank("z", 7)
                 nc.tensor.matmul_mx(
                     out=live["z", gate, x][:],
                     lhsT=w_codes[:, first : first + P].bitcast(FP8X4),
@@ -147,9 +147,9 @@ def tile_blockgrucell_pb_t_kernel(tc, y_dyn, deter, gru_W, gru_b, out):
                 )
 
         def gates(x):
-            live["reset", x] = strip_tile("reset", 3)
-            live["update", x] = strip_tile("update", 5)
-            live["product", x] = strip_tile("product", 3)
+            live["reset", x] = strip_tile("reset", 4)
+            live["update", x] = strip_tile("update", 8)
+            live["product", x] = strip_tile("product", 4)
             nc.scalar.activation(
                 out=live["reset", x][:], in_=live["z", GATE_R, x][:], func=ACT.Sigmoid, bias=bias_of(GATE_R, x)
             )
@@ -166,7 +166,7 @@ def tile_blockgrucell_pb_t_kernel(tc, y_dyn, deter, gru_W, gru_b, out):
             )
 
         def candidate(x):
-            live["cand", x] = strip_tile("cand", 3)
+            live["cand", x] = strip_tile("cand", 8)
             nc.scalar.activation(out=live["cand", x][:], in_=live["product", x][:], func=ACT.Tanh)
 
         def transpose_deter(pair):
@@ -178,8 +178,8 @@ def tile_blockgrucell_pb_t_kernel(tc, y_dyn, deter, gru_W, gru_b, out):
                 nc.tensor.transpose(live["deterT", pair][:, P * i : P * i + P], words[:, src : src + P], ident[:])
 
         def blend(x):
-            live["diff", x] = strip_tile("diff", 3)
-            live["step", x] = strip_tile("step", 5)
+            live["diff", x] = strip_tile("diff", 8)
+            live["step", x] = strip_tile("step", 8)
 
             def subtract(part):
                 nc.vector.tensor_tensor(
@@ -209,7 +209,7 @@ def tile_blockgrucell_pb_t_kernel(tc, y_dyn, deter, gru_W, gru_b, out):
 
         def open_sum(x):
             g, h, slots = x // 4, x // 2 % 2, slice(2 * (x % 2), 2 * (x % 2) + 2)
-            live["back", x] = bank("back", 2) if x < STRIPS - 4 else bank("z", 4)
+            live["back", x] = bank("z", 7) if x < STRIPS - 4 else bank("z", 7)
             rows = d_sb[g][:].rearrange("p (i c) -> p i c", i=4)[:, slots, 256 * h : 256 * h + 256]
             nc.tensor.matmul(
                 live["back", x][:].rearrange("p (i e q) -> p i e q", i=2, e=2),
@@ -222,7 +222,7 @@ def tile_blockgrucell_pb_t_kernel(tc, y_dyn, deter, gru_W, gru_b, out):
         def transpose_back(x):
             even = x - x % 2
             if x not in SUMMED:
-                live["back", x] = bank("back", 2)
+                live["back", x] = bank("z", 7)
             for i in range(2):
                 slot = 2 * (x % 2) + i
                 for e in range(2):
@@ -238,7 +238,7 @@ def tile_blockgrucell_pb_t_kernel(tc, y_dyn, deter, gru_W, gru_b, out):
         def finish(x):
             g, h, slots = x // 4, x // 2 % 2, slice(2 * (x % 2), 2 * (x % 2) + 2)
             cols = slice(256 * h, 256 * h + 256)
-            result = strip_tile("result", 8)
+            result = strip_tile("result", 16)
             back = live["back", x][:].rearrange("p (i e q) -> p i q e", i=2, e=2)
             total = result[:].rearrange("p (i q e) -> p i q e", i=2, e=2)
             if x in SUMMED:

@@ -52,15 +52,25 @@ def tile_blockgrucell_pb_t_kernel(tc, y_dyn, deter, gru_W, gru_b, out):
         y_sb = [keep.tile([P, 4 * 512], BF16, name="y%d" % g) for g in range(ROUNDS)]
         d_sb = [keep.tile([P, 4 * 512], BF16, name="d%d" % g) for g in range(ROUNDS)]
         w_raw = {}
-        for half in range(2):
-            cols = slice(1024 * half, 1024 * half + 1024)
-            nc.sync.dma_start(out=y_sb[0][:, cols], in_=y_rows[0][:, cols])
+        def load_y0(first, width):
+            nc.sync.dma_start(out=y_sb[0][:, first : first + width], in_=y_rows[0][:, first : first + width])
+
+        def load_weights(h, gate):
+            cols = slice(512 * gate + 256 * h, 512 * gate + 256 * h + 256)
+            w_raw[h, gate] = keep.tile([P, 4, 256], BF16, name="w_raw_%d%d" % (h, gate))
+            nc.sync.dma_start(out=w_raw[h, gate][:], in_=gru_W[0, :, cols].rearrange("(q t) c -> q t c", t=4))
+
+        load_y0(0, 512)
+        load_y0(512, 512)
+        load_weights(0, GATE_R)
         nc.sync.dma_start(out=b_rows[0:6, :], in_=gru_b.rearrange("(m c) -> m c", c=256))
-        for h in range(2):
-            for gate in (GATE_R, GATE_U, GATE_C):
-                cols = slice(512 * gate + 256 * h, 512 * gate + 256 * h + 256)
-                w_raw[h, gate] = keep.tile([P, 4, 256], BF16, name="w_raw_%d%d" % (h, gate))
-                nc.sync.dma_start(out=w_raw[h, gate][:], in_=gru_W[0, :, cols].rearrange("(q t) c -> q t c", t=4))
+        load_y0(1024, 512)
+        load_y0(1536, 512)
+        load_weights(0, GATE_U)
+        load_weights(0, GATE_C)
+        load_weights(1, GATE_R)
+        load_weights(1, GATE_U)
+        load_weights(1, GATE_C)
         for g in range(ROUNDS):
             if g + 1 < ROUNDS:
                 nc.sync.dma_start(out=y_sb[g + 1][:], in_=y_rows[g + 1])
@@ -114,10 +124,20 @@ def tile_blockgrucell_pb_t_kernel(tc, y_dyn, deter, gru_W, gru_b, out):
             if half == 0:
                 live["y_grouped", g] = work.tile([P, 4 * N], BF16, name="y_grouped", tag="y_grouped", bufs=2, align_bytes=256)
             words = live["y_grouped", g][:].bitcast(F32).rearrange("p (n u) -> p n u", u=2)
-            copy = nc.vector.tensor_copy if half == 1 and 0 < g < 5 else nc.scalar.copy
+            copy = nc.vector.tensor_copy if half == 1 and 0 < g < 3 else nc.scalar.copy
             copy(
                 out=words[:, 256 * half : 256 * half + 256, :].rearrange("p (i r) u -> p i r u", i=2),
                 in_=live["yT", g, half][:].rearrange("p (i u r) -> p i r u", i=2, u=2),
+            )
+
+        def regroup_y0(slot):
+            half, i = slot // 2, slot % 2
+            if slot == 0:
+                live["y_grouped", 0] = work.tile([P, 4 * N], BF16, name="y_grouped", tag="y_grouped", bufs=2, align_bytes=256)
+            words = live["y_grouped", 0][:].bitcast(F32).rearrange("p (n u) -> p n u", u=2)
+            nc.scalar.copy(
+                out=words[:, 128 * slot : 128 * slot + 128, :],
+                in_=live["yT", 0, half][:].rearrange("p (i u r) -> p i r u", i=2, u=2)[:, i],
             )
 
         def quantise_y(g, half):
@@ -131,9 +151,9 @@ def tile_blockgrucell_pb_t_kernel(tc, y_dyn, deter, gru_W, gru_b, out):
                 in_=live["y_grouped", g][:, 1024 * half : 1024 * half + 1024],
             )
 
-        def project(x):
+        def project(x, gates=(GATE_R, GATE_U, GATE_C)):
             g, h, e = x // 4, x // 2 % 2, x % 2
-            for gate in (GATE_R, GATE_U, GATE_C):
+            for gate in gates:
                 first = 256 * (3 * h + gate) + P * e
                 live["z", gate, x] = bank("z", 7)
                 nc.tensor.matmul_mx(
@@ -146,16 +166,18 @@ def tile_blockgrucell_pb_t_kernel(tc, y_dyn, deter, gru_W, gru_b, out):
                     stop=True,
                 )
 
-        def gates(x):
+        def sigmoids(x):
             live["reset", x] = strip_tile("reset", 4)
             live["update", x] = strip_tile("update", 8)
-            live["product", x] = strip_tile("product", 4)
             nc.scalar.activation(
                 out=live["reset", x][:], in_=live["z", GATE_R, x][:], func=ACT.Sigmoid, bias=bias_of(GATE_R, x)
             )
             nc.scalar.activation(
                 out=live["update", x][:], in_=live["z", GATE_U, x][:], func=ACT.Sigmoid, bias=bias_of(GATE_U, x)
             )
+
+        def product(x):
+            live["product", x] = strip_tile("product", 4)
             nc.vector.scalar_tensor_tensor(
                 out=live["product", x][:],
                 in0=live["z", GATE_C, x][:],
@@ -241,8 +263,15 @@ def tile_blockgrucell_pb_t_kernel(tc, y_dyn, deter, gru_W, gru_b, out):
             result = strip_tile("result", 16)
             back = live["back", x][:].rearrange("p (i e q) -> p i q e", i=2, e=2)
             total = result[:].rearrange("p (i q e) -> p i q e", i=2, e=2)
+            if x == STRIPS - 1:
+                for i in range(2):
+                    nc.vector.tensor_copy(out=total[:, i], in_=back[:, i])
+                    nc.sync.dma_start(
+                        out=o_rows[g][:, 2 + i, cols], in_=result[:, 256 * i : 256 * i + 256]
+                    )
+                return
             if x in SUMMED:
-                (nc.vector.tensor_copy if x in (31,) else nc.scalar.copy)(out=total, in_=back)
+                nc.scalar.copy(out=total, in_=back)
             else:
                 nc.vector.tensor_tensor(
                     out=total,
@@ -253,21 +282,38 @@ def tile_blockgrucell_pb_t_kernel(tc, y_dyn, deter, gru_W, gru_b, out):
             nc.sync.dma_start(out=o_rows[g][:, slots, cols], in_=result[:].rearrange("p (i c) -> p i c", i=2))
 
         transpose_y(0, 0)
-        transpose_y(0, 1)
         make_bias()
-        regroup_y(0, 0)
-        regroup_y(0, 1)
+        transpose_y(0, 1)
+        regroup_y0(0)
+        regroup_y0(1)
+        regroup_y0(2)
+        regroup_y0(3)
         regroup_weights(nc.vector.tensor_copy, 0, GATE_R)
-        quantise_weights(0, GATE_R)
         quantise_y(0, 0)
+        quantise_weights(0, GATE_R)
         quantise_y(0, 1)
         regroup_weights(nc.scalar.copy, 0, GATE_U)
         regroup_weights(nc.vector.tensor_copy, 0, GATE_C)
         quantise_weights(0, GATE_U)
         quantise_weights(0, GATE_C)
-        for gate in (GATE_R, GATE_U, GATE_C):
-            regroup_weights(nc.vector.tensor_copy, 1, gate)
-            quantise_weights(1, gate)
+        project(0, (GATE_R, GATE_U))
+        project(1, (GATE_R, GATE_U))
+        project(0, (GATE_C,))
+        project(1, (GATE_C,))
+        sigmoids(0)
+        sigmoids(1)
+        transpose_y(1, 0)
+        regroup_weights(nc.vector.tensor_copy, 1, GATE_R)
+        quantise_weights(1, GATE_R)
+        product(0)
+        product(1)
+        regroup_y(1, 0)
+        transpose_deter(0)
+        transpose_y(1, 1)
+        regroup_weights(nc.vector.tensor_copy, 1, GATE_U)
+        quantise_weights(1, GATE_U)
+        regroup_weights(nc.vector.tensor_copy, 1, GATE_C)
+        quantise_weights(1, GATE_C)
 
         def in_range(x):
             return 0 <= x < STRIPS
@@ -278,12 +324,13 @@ def tile_blockgrucell_pb_t_kernel(tc, y_dyn, deter, gru_W, gru_b, out):
                     if s == max(4 * g - 7 + 2 * half, -2):
                         stage(g, half)
 
-        for s in range(-2, STRIPS + 4):
+        for s in range(0, STRIPS + 4):
             if in_range(s - 1):
                 blend(s - 1)
             y_stage(quantise_y, s - 2)
-            if in_range(s + 1):
-                gates(s + 1)
+            if 2 <= s + 1 < STRIPS:
+                sigmoids(s + 1)
+                product(s + 1)
             y_stage(regroup_y, s - 1)
             if in_range(s - 4) and s < STRIPS - 2:
                 finish(s - 4)
@@ -297,7 +344,7 @@ def tile_blockgrucell_pb_t_kernel(tc, y_dyn, deter, gru_W, gru_b, out):
             if in_range(s + 2):
                 project(s + 2)
             y_stage(transpose_y, s)
-            if in_range(s) and s % 2 == 0:
+            if 0 < s < STRIPS and s % 2 == 0:
                 transpose_deter(s // 2)
             if s - 3 in SUMMED[:2]:
                 open_sum(s - 3)

from contextlib import ExitStack

import concourse.mybir as mybir
from concourse.masks import make_identity

FLOPS = 2 * 4096 * 512 * 1536

F32 = mybir.dt.float32
BF16 = mybir.dt.bfloat16
U32 = mybir.dt.uint32
U8 = mybir.dt.uint8
FP8X4 = mybir.dt.float8_e4m3fn_x4
ACT = mybir.ActivationFunctionType
ALU = mybir.AluOpType

P = 128
N = 512
ROUNDS = 8
STRIPS = 4 * ROUNDS
SUMMED = (26, 27, 28, 29, 30, 31)
GATE_R, GATE_C, GATE_U = 0, 1, 2


def tile_blockgrucell_pb_t_kernel(tc, y_dyn, deter, gru_W, gru_b, out):
    nc = tc.nc
    y_rows = y_dyn.rearrange("(g p i) k -> g p (i k)", p=P, i=4)
    d_rows = deter.rearrange("(g p i) c -> g p (i c)", p=P, i=4)
    o_rows = out.rearrange("(g p i) c -> g p i c", p=P, i=4)

    with ExitStack() as ctx:
        keep = ctx.enter_context(tc.tile_pool(name="keep", bufs=1))
        work = ctx.enter_context(tc.tile_pool(name="work", bufs=3))
        psum = ctx.enter_context(tc.psum_pool(name="psum", bufs=1))
        ctx.enter_context(tc.manual_schedule())

        def bank(tag, bufs):
            return psum.tile([P, N], F32, name=tag, tag=tag, bufs=bufs)

        def strip_tile(tag, bufs):
            return work.tile([P, N], F32, name=tag, tag=tag, bufs=bufs)

        ident = keep.tile([P, P], F32, name="ident")
        make_identity(nc, ident[:])
        b_rows = keep.tile([P, 256], BF16, name="b_rows")
        nc.vector.memset(b_rows[:], 0.0)
        warm = keep.tile([P, 2], F32, name="warm")
        nc.vector.memset(warm[:], 0.0)
        ident_bf16 = keep.tile([P, P], BF16, name="ident_bf16")
        nc.vector.tensor_copy(out=ident_bf16[:], in_=ident[:])
        nc.scalar.activation(out=warm[:, 1:2], in_=warm[:, 0:1], func=ACT.Sigmoid)

        y_sb = [keep.tile([P, 4 * 512], BF16, name="y%d" % g) for g in range(ROUNDS)]
        d_sb = [keep.tile([P, 4 * 512], BF16, name="d%d" % g) for g in range(ROUNDS)]
        w_raw = {}
        def load_y0(first, width):
            nc.sync.dma_start(out=y_sb[0][:, first : first + width], in_=y_rows[0][:, first : first + width])

        def load_weights(h, gate):
            cols = slice(512 * gate + 256 * h, 512 * gate + 256 * h + 256)
            w_raw[h, gate] = keep.tile([P, 4, 256], BF16, name="w_raw_%d%d" % (h, gate))
            nc.sync.dma_start(out=w_raw[h, gate][:], in_=gru_W[0, :, cols].rearrange("(q t) c -> q t c", t=4))

        load_y0(0, 512)
        load_y0(512, 512)
        load_weights(0, GATE_R)
        nc.sync.dma_start(out=b_rows[0:6, :], in_=gru_b.rearrange("(m c) -> m c", c=256))
        load_y0(1024, 512)
        load_y0(1536, 512)
        load_weights(0, GATE_U)
        load_weights(0, GATE_C)
        load_weights(1, GATE_R)
        load_weights(1, GATE_U)
        load_weights(1, GATE_C)
        for g in range(ROUNDS):
            if g + 1 < ROUNDS:
                nc.sync.dma_start(out=y_sb[g + 1][:], in_=y_rows[g + 1])
            nc.sync.dma_start(out=d_sb[g][:], in_=d_rows[g])

        bias = keep.tile([P, 12], F32, name="bias")

        def make_bias():
            b_bank = bank("z", 7)
            nc.tensor.transpose(b_bank[:, 0:P], b_rows[:].bitcast(F32), ident[:])
            nc.vector.tensor_copy(out=bias[:], in_=b_bank[:].bitcast(BF16)[:, 0:12])
            nc.vector.tensor_scalar_add(
                out=bias[:, 4 * GATE_U : 4 * GATE_U + 4], in0=bias[:, 4 * GATE_U : 4 * GATE_U + 4], scalar1=-1.0
            )

        def bias_of(gate, x):
            column = 4 * gate + x % 4
            return bias[:, column : column + 1]

        w_grouped = keep.tile([P, 6 * 1024], BF16, name="w_grouped", align_bytes=256)
        w_codes = keep.tile([P, 6 * 256], U32, name="w_codes", align_bytes=256)
        w_scales = keep.tile([P, 6 * 256], U8, name="w_scales", align_bytes=256)

        def regroup_weights(copy, h, gate):
            slot = 3 * h + gate
            copy(
                out=w_grouped[:, 1024 * slot : 1024 * slot + 1024].rearrange("p (e c i t) -> p e c t i", e=2, i=4, t=4),
                in_=w_raw[h, gate][:].rearrange("p t (c i e) -> p e c t i", i=4, e=2),
            )

        def quantise_weights(h, gate):
            slot = 3 * h + gate
            nc.vector.quantize_mx(
                out=w_codes[:, 256 * slot : 256 * slot + 256].bitcast(FP8X4),
                scales=w_scales[:, 256 * slot : 256 * slot + 256],
                in_=w_grouped[:, 1024 * slot : 1024 * slot + 1024],
            )

        live = {}

        def transpose_y(g, half):
            live["yT", g, half] = bank("z", 7) if g == 0 else bank("z", 7)
            words = y_sb[g][:].bitcast(F32)
            for i in range(2):
                for u in range(2):
                    row = 256 * (2 * half + i)
                    dst = 128 * (2 * i + u)
                    nc.tensor.transpose(live["yT", g, half][:, dst : dst + P], words[:, row + u : row + 256 : 2], ident[:])

        def regroup_y(g, half):
            if half == 0:
                live["y_grouped", g] = work.tile([P, 4 * N], BF16, name="y_grouped", tag="y_grouped", bufs=2, align_bytes=256)
            words = live["y_grouped", g][:].bitcast(F32).rearrange("p (n u) -> p n u", u=2)
            copy = nc.vector.tensor_copy if half == 1 and 0 < g < 3 else nc.scalar.copy
            copy(
                out=words[:, 256 * half : 256 * half + 256, :].rearrange("p (i r) u -> p i r u", i=2),
                in_=live["yT", g, half][:].rearrange("p (i u r) -> p i r u", i=2, u=2),
            )

        def regroup_y0(slot):
            half, i = slot // 2, slot % 2
            if slot == 0:
                live["y_grouped", 0] = work.tile([P, 4 * N], BF16, name="y_grouped", tag="y_grouped", bufs=2, align_bytes=256)
            words = live["y_grouped", 0][:].bitcast(F32).rearrange("p (n u) -> p n u", u=2)
            nc.scalar.copy(
                out=words[:, 128 * slot : 128 * slot + 128, :],
                in_=live["yT", 0, half][:].rearrange("p (i u r) -> p i r u", i=2, u=2)[:, i],
            )

        def quantise_y(g, half):
            if half == 0:
                live["y_codes", g] = work.tile([P, N], U32, name="y_codes", tag="y_codes", bufs=2, align_bytes=256)
                live["y_scales", g] = work.tile([P, N], U8, name="y_scales", tag="y_scales", bufs=2, align_bytes=256)
            cols = slice(256 * half, 256 * half + 256)
            nc.vector.quantize_mx(
                out=live["y_codes", g][:, cols].bitcast(FP8X4),
                scales=live["y_scales", g][:, cols],
                in_=live["y_grouped", g][:, 1024 * half : 1024 * half + 1024],
            )

        def project(x, gates=(GATE_R, GATE_U, GATE_C)):
            g, h, e = x // 4, x // 2 % 2, x % 2
            for gate in gates:
                first = 256 * (3 * h + gate) + P * e
                live["z", gate, x] = bank("z", 7)
                nc.tensor.matmul_mx(
                    out=live["z", gate, x][:],
                    lhsT=w_codes[:, first : first + P].bitcast(FP8X4),
                    lhsT_scale=w_scales[:, first : first + P],
                    rhs=live["y_codes", g][:].bitcast(FP8X4),
                    rhs_scale=live["y_scales", g][:],
                    start=True,
                    stop=True,
                )

        def sigmoids(x):
            live["reset", x] = strip_tile("reset", 4)
            live["update", x] = strip_tile("update", 8)
            nc.scalar.activation(
                out=live["reset", x][:], in_=live["z", GATE_R, x][:], func=ACT.Sigmoid, bias=bias_of(GATE_R, x)
            )
            nc.scalar.activation(
                out=live["update", x][:], in_=live["z", GATE_U, x][:], func=ACT.Sigmoid, bias=bias_of(GATE_U, x)
            )

        def product(x):
            live["product", x] = strip_tile("product", 4)
            nc.vector.scalar_tensor_tensor(
                out=live["product", x][:],
                in0=live["z", GATE_C, x][:],
                scalar=bias_of(GATE_C, x),
                in1=live["reset", x][:],
                op0=ALU.add,
                op1=ALU.mult,
            )

        def candidate(x):
            live["cand", x] = strip_tile("cand", 8)
            nc.scalar.activation(out=live["cand", x][:], in_=live["product", x][:], func=ACT.Tanh)

        def transpose_deter(pair):
            g, h = pair // 2, pair % 2
            live["deterT", pair] = bank("deterT", 1)
            words = d_sb[g][:].bitcast(F32)
            for i in range(4):
                src = 256 * i + P * h
                nc.tensor.transpose(live["deterT", pair][:, P * i : P * i + P], words[:, src : src + P], ident[:])

        def blend(x):
            live["diff", x] = strip_tile("diff", 8)
            live["step", x] = strip_tile("step", 8)

            def subtract(part):
                nc.vector.tensor_tensor(
                    out=live["diff", x][:, part],
                    in0=live["cand", x][:, part],
                    in1=live["deterT", x // 2][:].bitcast(BF16).rearrange("p (n e) -> p e n", e=2)[:, x % 2, part],
                    op=ALU.subtract,
                )

            def multiply(engine, x, part):
                engine.tensor_tensor(
                    out=live["step", x][:, part], in0=live["update", x][:, part], in1=live["diff", x][:, part], op=ALU.mult
                )

            whole, halves = slice(0, 512), (slice(0, 256), slice(256, 512))
            if x < STRIPS - 2:
                subtract(whole)
                multiply(nc.gpsimd, x, whole)
            elif x == STRIPS - 2:
                subtract(whole)
            else:
                multiply(nc.vector, x - 1, whole)
                for part in halves:
                    subtract(part)
                for part in halves:
                    multiply(nc.vector, x, part)

        def open_sum(x):
            g, h, slots = x // 4, x // 2 % 2, slice(2 * (x % 2), 2 * (x % 2) + 2)
            live["back", x] = bank("z", 7) if x < STRIPS - 4 else bank("z", 7)
            rows = d_sb[g][:].rearrange("p (i c) -> p i c", i=4)[:, slots, 256 * h : 256 * h + 256]
            nc.tensor.matmul(
                live["back", x][:].rearrange("p (i e q) -> p i e q", i=2, e=2),
                lhsT=ident_bf16[:],
                rhs=rows.rearrange("p i (q e) -> p i e q", e=2),
                start=True,
                stop=False,
            )

        def transpose_back(x):
            even = x - x % 2
            if x not in SUMMED:
                live["back", x] = bank("z", 7)
            for i in range(2):
                slot = 2 * (x % 2) + i
                for e in range(2):
                    dst = live["back", x][:, P * (2 * i + e) : P * (2 * i + e) + P]
                    step = live["step", even + e][:, P * slot : P * slot + P]
                    if x in SUMMED:
                        nc.tensor.matmul(
                            dst, lhsT=step, rhs=ident[:], start=False, stop=i == 1 and e == 1, is_transpose=True
                        )
                    else:
                        nc.tensor.transpose(dst, step, ident[:])

        def finish(x):
            g, h, slots = x // 4, x // 2 % 2, slice(2 * (x % 2), 2 * (x % 2) + 2)
            cols = slice(256 * h, 256 * h + 256)
            result = strip_tile("result", 16)
            back = live["back", x][:].rearrange("p (i e q) -> p i q e", i=2, e=2)
            total = result[:].rearrange("p (i q e) -> p i q e", i=2, e=2)
            if x == STRIPS - 1:
                for i in range(2):
                    nc.vector.tensor_copy(out=total[:, i], in_=back[:, i])
                    nc.sync.dma_start(
                        out=o_rows[g][:, 2 + i, cols], in_=result[:, 256 * i : 256 * i + 256]
                    )
                return
            if x in SUMMED:
                nc.scalar.copy(out=total, in_=back)
            else:
                nc.vector.tensor_tensor(
                    out=total,
                    in0=back,
                    in1=d_sb[g][:].rearrange("p (i c) -> p i c", i=4)[:, slots, cols].rearrange("p i (q e) -> p i q e", e=2),
                    op=ALU.add,
                )
            nc.sync.dma_start(out=o_rows[g][:, slots, cols], in_=result[:].rearrange("p (i c) -> p i c", i=2))

        transpose_y(0, 0)
        make_bias()
        transpose_y(0, 1)
        regroup_y0(0)
        regroup_y0(1)
        regroup_y0(2)
        regroup_y0(3)
        regroup_weights(nc.vector.tensor_copy, 0, GATE_R)
        quantise_y(0, 0)
        quantise_weights(0, GATE_R)
        quantise_y(0, 1)
        regroup_weights(nc.scalar.copy, 0, GATE_U)
        regroup_weights(nc.vector.tensor_copy, 0, GATE_C)
        quantise_weights(0, GATE_U)
        quantise_weights(0, GATE_C)
        project(0, (GATE_R, GATE_U))
        project(1, (GATE_R, GATE_U))
        project(0, (GATE_C,))
        project(1, (GATE_C,))
        sigmoids(0)
        sigmoids(1)
        transpose_y(1, 0)
        regroup_weights(nc.vector.tensor_copy, 1, GATE_R)
        quantise_weights(1, GATE_R)
        product(0)
        product(1)
        regroup_y(1, 0)
        transpose_deter(0)
        transpose_y(1, 1)
        regroup_weights(nc.vector.tensor_copy, 1, GATE_U)
        quantise_weights(1, GATE_U)
        regroup_weights(nc.vector.tensor_copy, 1, GATE_C)
        quantise_weights(1, GATE_C)

        def in_range(x):
            return 0 <= x < STRIPS

        def y_stage(stage, s):
            for g in range(1, ROUNDS):
                for half in range(2):
                    if s == max(4 * g - 7 + 2 * half, -2):
                        stage(g, half)

        for s in range(0, STRIPS + 4):
            if in_range(s - 1):
                blend(s - 1)
            y_stage(quantise_y, s - 2)
            if 2 <= s + 1 < STRIPS:
                sigmoids(s + 1)
                product(s + 1)
            y_stage(regroup_y, s - 1)
            if in_range(s - 4) and s < STRIPS - 2:
                finish(s - 4)
            if in_range(s):
                candidate(s)
            if s == STRIPS - 1:
                finish(26)
                finish(27)
            if in_range(s - 4) and s >= STRIPS:
                finish(s - 4)
            if in_range(s + 2):
                project(s + 2)
            y_stage(transpose_y, s)
            if 0 < s < STRIPS and s % 2 == 0:
                transpose_deter(s // 2)
            if s - 3 in SUMMED[:2]:
                open_sum(s - 3)
            if s == STRIPS - 1:
                for x in SUMMED[2:]:
                    open_sum(x)
            if in_range(s - 3):
                transpose_back(s - 3)
